import numpy as np
import ml_dtypes


def mxq(x, axis, fmt="e4m3"):
    dtype, down = {"e4m3": (ml_dtypes.float8_e4m3fn, 7), "e5m2": (ml_dtypes.float8_e5m2, 14)}[fmt]
    v = np.moveaxis(np.asarray(x, np.float32).astype(ml_dtypes.bfloat16).astype(np.float64), axis, -1)
    blocks = v.reshape(v.shape[:-1] + (-1, 32))
    amax = np.abs(blocks).max(-1, keepdims=True)
    byte = np.maximum(np.where(amax > 0, np.frexp(amax)[1] - 1 + 127, 0) - down, 1)
    scale = np.exp2(byte - 127.0)
    codes = (blocks / scale).astype(np.float32).astype(dtype).astype(np.float64)
    return np.moveaxis((codes * scale).reshape(v.shape), -1, axis)


WIDE = False


def mx_kscale(k):
    if not WIDE:
        return np.ones(k)
    levels = np.array([10, -10, 5, -5, 0])
    a = np.random.permutation(np.resize(levels, k // 512 * 4)).reshape(k // 512, 4)
    idx = np.arange(k)
    return np.exp2(a[idx // 512, idx % 128 // 32])


BF16 = ml_dtypes.bfloat16


def bf(x):
    return np.asarray(x, np.float32).astype(BF16)


def f64(x):
    return np.asarray(x).astype(np.float64)


B, N, D, H, DH, GD = 3, 2048, 512, 4, 128, 128
INNER = H * DH
LN_EPS = 1e-5


def silu(v):
    return v / (1.0 + np.exp(-v))


def sigmoid(v):
    return 1.0 / (1.0 + np.exp(-v))


def setup_inputs():
    t = mx_kscale(INNER)
    theta = (10000.0 ** (-2.0 / INNER * np.arange(INNER)) * (1.0 + 0.1 * np.random.standard_normal(INNER))).reshape(H, 1, DH)
    ang = theta * np.arange(N).reshape(1, N, 1)
    tab = np.concatenate([np.cos(ang), np.sin(ang)], axis=-1)
    qs = silu(np.random.standard_normal((B, H, N, DH)))
    mu, m2 = qs.mean(), (qs ** 2).mean()
    kv_mean = mu * mu * tab.sum(1)
    kv_spread = np.sqrt((m2 * m2 - mu ** 4) * (tab ** 2).sum(1))
    kv = (kv_mean[None, :, :, None] + kv_spread[None, :, :, None] * np.random.standard_normal((B, H, 2 * DH, DH))) / np.sqrt(2 * DH)
    return {"q_rot": bf(np.concatenate([qs, qs], axis=-1) * tab[None] / np.sqrt(2 * DH)),
            "kv": bf(kv),
            "g_low": bf(np.random.standard_normal((B, N, GD))),
            "w_g2": bf(np.random.standard_normal((GD, INNER)) / np.sqrt(GD)),
            "ln_gamma": bf((1.0 + 0.1 * np.random.standard_normal(INNER)) * t),
            "ln_beta": bf(0.1 * np.random.standard_normal(INNER) * t),
            "w_out": bf(np.random.standard_normal((INNER, D)) / np.sqrt(INNER) / t[:, None]),
            "b_out": bf(0.1 * np.random.standard_normal(D))}


def reference(q_rot, kv, g_low, w_g2, ln_gamma, ln_beta, w_out, b_out):
    o = f64(q_rot) @ f64(kv)
    o = o.transpose(0, 2, 1, 3).reshape(B, N, INNER)
    mu = o.mean(-1, keepdims=True)
    var = ((o - mu) ** 2).mean(-1, keepdims=True)
    y = (o - mu) / np.sqrt(var + LN_EPS) * f64(ln_gamma) + f64(ln_beta)
    gate = sigmoid(f64(g_low) @ f64(w_g2))
    h = y * gate
    return (mxq(h, 2, "e4m3") @ mxq(f64(w_out), 0, "e4m3")) + f64(b_out)

@@ -1,0 +1,262 @@
+from contextlib import ExitStack
+
+import concourse.mybir as mybir
+from concourse.masks import make_identity
+
+F32 = mybir.dt.float32
+BF16 = mybir.dt.bfloat16
+U32 = mybir.dt.uint32
+U8 = mybir.dt.uint8
+FP8X4 = mybir.dt.float8_e4m3fn_x4
+ACT = mybir.ActivationFunctionType
+ALU = mybir.AluOpType
+
+P = 128
+BATCH, TOKENS, HEADS, QK, DH, GD = 3, 2048, 4, 256, 128, 128
+INNER = HEADS * DH
+D_OUT = 512
+LN_EPS = 1e-5
+PACK = 4
+PAIR = 2
+
+TILES_PER_CHUNK = 4
+CHUNK = TILES_PER_CHUNK * P
+CHUNKS_PER_BATCH = TOKENS // CHUNK
+CHUNKS = BATCH * CHUNKS_PER_BATCH
+TILES = CHUNKS * TILES_PER_CHUNK
+
+FLOPS = 2 * BATCH * TOKENS * (HEADS * QK * DH + GD * INNER + INNER * D_OUT)
+
+
+def tile_linearattention_pb_t_kernel(
+    tc, q_rot, kv, g_low, w_g2, ln_gamma, ln_beta, w_out, b_out, out
+):
+    nc = tc.nc
+    with ExitStack() as ctx:
+        const = ctx.enter_context(tc.tile_pool(name="const", bufs=1))
+        q_pool = ctx.enter_context(tc.tile_pool(name="q_pool", bufs=CHUNKS))
+        g_pool = ctx.enter_context(tc.tile_pool(name="g_pool", bufs=BATCH))
+        work2 = ctx.enter_context(tc.tile_pool(name="work2", bufs=2))
+        work3 = ctx.enter_context(tc.tile_pool(name="work3", bufs=3))
+        psum1 = ctx.enter_context(tc.psum_pool(name="psum1", bufs=1))
+        psum3 = ctx.enter_context(tc.psum_pool(name="psum3", bufs=3))
+
+        q_sb = []
+        g_sb = []
+        kv_sb = const.tile([P, BATCH, HEADS, PAIR, DH], BF16)
+        w_g2_sb = const.tile([P, INNER], BF16)
+        ln_rows = const.tile([P, P], BF16)
+        w_raw = const.tile([P, PACK, D_OUT], BF16)
+        bias_bc = const.tile([P, D_OUT], BF16)
+
+        def load_q(c):
+            b, cb = divmod(c, CHUNKS_PER_BATCH)
+            q_chunk = q_pool.tile([P, HEADS, TILES_PER_CHUNK, QK], BF16, name="q_chunk")
+            nc.sync.dma_start(
+                out=q_chunk[:].rearrange("p h j k -> p h (j k)"),
+                in_=q_rot[b, :, cb * CHUNK : (cb + 1) * CHUNK, :].rearrange(
+                    "h (p j) k -> p h (j k)", j=TILES_PER_CHUNK
+                ),
+            )
+            q_sb.append(q_chunk)
+
+        def load_kv_and_g(b):
+            nc.sync.dma_start(
+                out=kv_sb[:, b].rearrange("w h e d -> w h (e d)"),
+                in_=kv[b].rearrange("h (w e) d -> w h (e d)", e=PAIR),
+            )
+            g_batch = g_pool.tile([P, CHUNKS_PER_BATCH, TILES_PER_CHUNK, GD], BF16, name="g_batch")
+            nc.sync.dma_start(
+                out=g_batch[:].rearrange("p c j k -> p c (j k)"),
+                in_=g_low[b].rearrange("(c p j) k -> p c (j k)", p=P, j=TILES_PER_CHUNK),
+            )
+            g_sb.append(g_batch)
+
+        nc.vector.memset(ln_rows[:], 0.0)
+
+        load_q(0)
+        load_kv_and_g(0)
+        nc.sync.dma_start(out=w_g2_sb[:], in_=w_g2)
+        nc.sync.dma_start(out=ln_rows[0:HEADS, :], in_=ln_gamma.rearrange("(t p) -> t p", p=P))
+        nc.sync.dma_start(
+            out=ln_rows[HEADS : 2 * HEADS, :], in_=ln_beta.rearrange("(t p) -> t p", p=P)
+        )
+        nc.sync.dma_start(out=w_raw[:], in_=w_out.rearrange("(t p) n -> p t n", p=P))
+        nc.sync.dma_start(out=bias_bc[:], in_=b_out.partition_broadcast(P))
+        for c in range(1, CHUNKS):
+            if c % CHUNKS_PER_BATCH == 0:
+                load_kv_and_g(c // CHUNKS_PER_BATCH)
+            load_q(c)
+
+        ident_f32 = const.tile([P, P], F32)
+        make_identity(nc, ident_f32[:])
+        ident_bf16 = const.tile([P, P], BF16)
+        make_identity(nc, ident_bf16[:])
+        neg_half = const.tile([P, 1], F32)
+        nc.vector.memset(neg_half[:], -0.5)
+
+        ln_cols_ps = psum1.tile([P, P], BF16, name="gT_ps")
+        nc.tensor.transpose(ln_cols_ps[:], ln_rows[:], ident_bf16[:])
+        ln_cols = const.tile([P, 2 * HEADS], F32)
+        nc.vector.tensor_copy(out=ln_cols[:], in_=ln_cols_ps[:, 0 : 2 * HEADS])
+
+        w_grouped = const.tile([P, D_OUT, PACK], BF16, align_bytes=64)
+        nc.vector.tensor_copy(out=w_grouped[:], in_=w_raw[:].rearrange("p t n -> p n t"))
+        w_codes = const.tile([P, D_OUT], U32, align_bytes=64)
+        w_scales = const.tile([P, D_OUT], U8, align_bytes=64)
+        nc.vector.quantize_mx(
+            out=w_codes[:].bitcast(FP8X4),
+            scales=w_scales[:],
+            in_=w_grouped[:].rearrange("p n t -> p (n t)"),
+        )
+
+        gT_sb, qT_sb, o_ps, mean_var, rstd = {}, {}, {}, {}, {}
+        z_sb, y_sb, gate_sb, h_sb, h_codes, h_scales, out_ps, out_sb = {}, {}, {}, {}, {}, {}, {}, {}
+
+        def place(i):
+            c, j = divmod(i, TILES_PER_CHUNK)
+            b, cb = divmod(c, CHUNKS_PER_BATCH)
+            return b, cb, c, j
+
+        def transpose_g(c):
+            b, cb = divmod(c, CHUNKS_PER_BATCH)
+            gT_ps = psum1.tile([P, CHUNK], BF16, name="gT_ps")
+            for j in range(TILES_PER_CHUNK):
+                nc.tensor.transpose(gT_ps[:, j * P : (j + 1) * P], g_sb[b][:, cb, j, :], ident_bf16[:])
+            gT_sb[c] = work2.tile([P, CHUNK], BF16, name="gT")
+            nc.scalar.copy(out=gT_sb[c][:], in_=gT_ps[:])
+
+        def transpose_q(i):
+            b, cb, c, j = place(i)
+            q_words = q_sb[c][:].bitcast(F32)
+            qT_ps = psum1.tile([P, HEADS * P], F32, name="qT_ps")
+            for h in range(HEADS):
+                nc.tensor.transpose(qT_ps[:, h * P : (h + 1) * P], q_words[:, h, j, :], ident_f32[:])
+            qT_sb[i] = work2.tile([P, HEADS * P * PAIR], BF16, name="qT")
+            nc.scalar.copy(out=qT_sb[i][:], in_=qT_ps[:].bitcast(BF16))
+
+        def attend(i):
+            b, cb, c, j = place(i)
+            o_ps[i] = psum3.tile([P, INNER], F32, name="o_ps")
+            for h in range(HEADS):
+                q_head = qT_sb[i][:, h * P * PAIR : (h + 1) * P * PAIR].rearrange(
+                    "w (n e) -> w n e", e=PAIR
+                )
+                for e in range(PAIR):
+                    nc.tensor.matmul(
+                        o_ps[i][:, h * DH : (h + 1) * DH],
+                        lhsT=q_head[:, :, e],
+                        rhs=kv_sb[:, b, h, e, :],
+                        start=(e == 0),
+                        stop=(e == PAIR - 1),
+                    )
+
+        def statistics(i):
+            stats = work3.tile([P, 6], F32, name="stats")
+            nc.vector.bn_stats(out=stats[:], in_=o_ps[i][:])
+            mean_var[i] = work3.tile([P, 2], F32, name="mean_var")
+            nc.vector.bn_aggr(out=mean_var[i][:], in_=stats[:])
+
+        def inverse_std(i):
+            var_eps = work3.tile([P, 1], F32, name="var_eps")
+            nc.gpsimd.tensor_scalar(
+                out=var_eps[:], in0=mean_var[i][:, 1:2], scalar1=LN_EPS, scalar2=1.0,
+                op0=ALU.add, op1=ALU.mult,
+            )
+            rstd[i] = work3.tile([P, 1], F32, name="rstd")
+            nc.gpsimd.tensor_tensor(out=rstd[i][:], in0=var_eps[:], in1=neg_half[:], op=ALU.pow)
+
+        def normalise(i):
+            z_sb[i] = work2.tile([P, INNER], F32, name="z")
+            nc.vector.tensor_scalar(
+                out=z_sb[i][:], in0=o_ps[i][:], scalar1=mean_var[i][:, 0:1], scalar2=rstd[i][:],
+                op0=ALU.subtract, op1=ALU.mult,
+            )
+
+        def scale_and_shift(i):
+            zT_ps = psum1.tile([P, HEADS, P], F32, name="zT_ps")
+            for t in range(HEADS):
+                nc.tensor.transpose(zT_ps[:, t, :], z_sb[i][:, t * DH : (t + 1) * DH], ident_f32[:])
+            y_sb[i] = work2.tile([P, HEADS, P], F32, name="y")
+            for t in range(HEADS):
+                nc.scalar.activation(
+                    out=y_sb[i][:, t, :], in_=zT_ps[:, t, :], func=ACT.Identity,
+                    scale=ln_cols[:, t : t + 1], bias=ln_cols[:, HEADS + t : HEADS + t + 1],
+                )
+
+        def gate(i):
+            b, cb, c, j = place(i)
+            gate_ps = psum1.tile([P, HEADS, P], F32, name="gate_ps")
+            for t in range(HEADS):
+                nc.tensor.matmul(
+                    gate_ps[:, t, :],
+                    lhsT=w_g2_sb[:, t * DH : (t + 1) * DH],
+                    rhs=gT_sb[c][:, j * P : (j + 1) * P],
+                    start=True,
+                    stop=True,
+                )
+            gate_sb[i] = work3.tile([P, HEADS, P], F32, name="gate_sb")
+            nc.scalar.activation(out=gate_sb[i][:], in_=gate_ps[:], func=ACT.Sigmoid)
+
+        def apply_gate(i):
+            h_sb[i] = work2.tile([P, P, PACK], BF16, name="h", align_bytes=64)
+            nc.gpsimd.tensor_tensor(
+                out=h_sb[i][:].rearrange("p (c r) t -> p c t r", r=4),
+                in0=y_sb[i][:].rearrange("p t (c r) -> p c t r", r=4),
+                in1=gate_sb[i][:].rearrange("p t (c r) -> p c t r", r=4),
+                op=ALU.mult,
+            )
+
+        def quantise(i):
+            h_codes[i] = work2.tile([P, P], U32, name="h_codes", align_bytes=64)
+            h_scales[i] = work2.tile([P, P], U8, name="h_scales", align_bytes=64)
+            nc.vector.quantize_mx(
+                out=h_codes[i][:].bitcast(FP8X4),
+                scales=h_scales[i][:],
+                in_=h_sb[i][:].rearrange("p n t -> p (n t)"),
+            )
+
+        def project(i):
+            out_ps[i] = psum1.tile([P, D_OUT], F32, name="out_ps")
+            nc.tensor.matmul_mx(
+                out=out_ps[i][:],
+                lhsT=h_codes[i][:].bitcast(FP8X4),
+                lhsT_scale=h_scales[i][:],
+                rhs=w_codes[:].bitcast(FP8X4),
+                rhs_scale=w_scales[:],
+                start=True,
+                stop=True,
+            )
+
+        def add_bias(i):
+            b, cb, c, j = place(i)
+            if j == 0:
+                out_sb[c] = work3.tile([P, TILES_PER_CHUNK, D_OUT], F32, name="out_sb")
+            nc.vector.tensor_tensor(out=out_sb[c][:, j, :], in0=out_ps[i][:], in1=bias_bc[:], op=ALU.add)
+            if j == TILES_PER_CHUNK - 1:
+                nc.sync.dma_start(
+                    out=out[b, cb * CHUNK : (cb + 1) * CHUNK, :].rearrange(
+                        "(p j) n -> p (j n)", j=TILES_PER_CHUNK
+                    ),
+                    in_=out_sb[c][:].rearrange("p j n -> p (j n)"),
+                )
+
+        def run(stage, i):
+            if 0 <= i < TILES:
+                stage(i)
+
+        with tc.manual_schedule():
+            for s in range(TILES + 5):
+                run(quantise, s - 5)
+                if s < TILES and s % TILES_PER_CHUNK == 0:
+                    transpose_g(s // TILES_PER_CHUNK)
+                run(transpose_q, s)
+                run(attend, s - 1)
+                run(statistics, s - 1)
+                run(inverse_std, s - 2)
+                run(normalise, s - 2)
+                run(scale_and_shift, s - 3)
+                run(gate, s - 2)
+                run(project, s - 5)
+                run(apply_gate, s - 4)
+                run(add_bias, s - 5)

@@ -200,7 +200,7 @@ def tile_linearattention_pb_t_kernel(
 
         def apply_gate(i):
             h_sb[i] = work2.tile([P, P, PACK], BF16, name="h", align_bytes=64)
-            nc.gpsimd.tensor_tensor(
+            nc.vector.tensor_tensor(
                 out=h_sb[i][:].rearrange("p (c r) t -> p c t r", r=4),
                 in0=y_sb[i][:].rearrange("p t (c r) -> p c t r", r=4),
                 in1=gate_sb[i][:].rearrange("p t (c r) -> p c t r", r=4),

@@ -110,8 +110,11 @@ def tile_linearattention_pb_t_kernel(
             in_=w_grouped[:].rearrange("p n t -> p (n t)"),
         )
 
-        gT_sb, qT_sb, o_ps, mean_var, rstd = {}, {}, {}, {}, {}
+        gT_sb, qT_sb, o_ps, stats, mean_var, rstd, shift = {}, {}, {}, {}, {}, {}, {}
         z_sb, y_sb, gate_sb, h_sb, h_codes, h_scales, out_ps, out_sb = {}, {}, {}, {}, {}, {}, {}, {}
+
+        def on_scalar(i):
+            return i % 2 == 1
 
         def place(i):
             c, j = divmod(i, TILES_PER_CHUNK)
@@ -151,11 +154,13 @@ def tile_linearattention_pb_t_kernel(
                         stop=(e == PAIR - 1),
                     )
 
+        def partial_statistics(i):
+            stats[i] = work3.tile([P, 6], F32, name="stats")
+            nc.vector.bn_stats(out=stats[i][:], in_=o_ps[i][:])
+
         def statistics(i):
-            stats = work3.tile([P, 6], F32, name="stats")
-            nc.vector.bn_stats(out=stats[:], in_=o_ps[i][:])
             mean_var[i] = work3.tile([P, 2], F32, name="mean_var")
-            nc.vector.bn_aggr(out=mean_var[i][:], in_=stats[:])
+            nc.vector.bn_aggr(out=mean_var[i][:], in_=stats[i][:])
 
         def inverse_std(i):
             var_eps = work3.tile([P, 1], F32, name="var_eps")
@@ -165,13 +170,25 @@ def tile_linearattention_pb_t_kernel(
             )
             rstd[i] = work3.tile([P, 1], F32, name="rstd")
             nc.gpsimd.tensor_tensor(out=rstd[i][:], in0=var_eps[:], in1=neg_half[:], op=ALU.pow)
+            if on_scalar(i):
+                shift[i] = work3.tile([P, 1], F32, name="shift")
+                nc.gpsimd.tensor_scalar(
+                    out=shift[i][:], in0=mean_var[i][:, 0:1], scalar1=rstd[i][:], scalar2=-1.0,
+                    op0=ALU.mult, op1=ALU.mult,
+                )
 
         def normalise(i):
             z_sb[i] = work2.tile([P, INNER], F32, name="z")
-            nc.vector.tensor_scalar(
-                out=z_sb[i][:], in0=o_ps[i][:], scalar1=mean_var[i][:, 0:1], scalar2=rstd[i][:],
-                op0=ALU.subtract, op1=ALU.mult,
-            )
+            if on_scalar(i):
+                nc.scalar.activation(
+                    out=z_sb[i][:], in_=o_ps[i][:], func=ACT.Identity,
+                    scale=rstd[i][:], bias=shift[i][:],
+                )
+            else:
+                nc.vector.tensor_scalar(
+                    out=z_sb[i][:], in0=o_ps[i][:], scalar1=mean_var[i][:, 0:1], scalar2=rstd[i][:],
+                    op0=ALU.subtract, op1=ALU.mult,
+                )
 
         def scale_and_shift(i):
             zT_ps = psum1.tile([P, HEADS, P], F32, name="zT_ps")
@@ -247,16 +264,17 @@ def tile_linearattention_pb_t_kernel(
 
         with tc.manual_schedule():
             for s in range(TILES + 5):
-                run(quantise, s - 5)
                 if s < TILES and s % TILES_PER_CHUNK == 0:
                     transpose_g(s // TILES_PER_CHUNK)
                 run(transpose_q, s)
                 run(attend, s - 1)
-                run(statistics, s - 1)
-                run(inverse_std, s - 2)
-                run(normalise, s - 2)
+                run(partial_statistics, s - 1)
+                run(apply_gate, s - 4)
                 run(scale_and_shift, s - 3)
+                run(inverse_std, s - 2)
+                run(statistics, s - 1)
+                run(normalise, s - 2)
                 run(gate, s - 2)
                 run(project, s - 5)
-                run(apply_gate, s - 4)
+                run(quantise, s - 4)
                 run(add_bias, s - 5)

@@ -18,12 +18,12 @@ D_OUT = 512
 LN_EPS = 1e-5
 PACK = 4
 PAIR = 2
+RUN = 4
 
-TILES_PER_CHUNK = 4
-CHUNK = TILES_PER_CHUNK * P
-CHUNKS_PER_BATCH = TOKENS // CHUNK
-CHUNKS = BATCH * CHUNKS_PER_BATCH
-TILES = CHUNKS * TILES_PER_CHUNK
+TILES_PER_BATCH = TOKENS // P
+TILES = BATCH * TILES_PER_BATCH
+GROUP = 4
+OUT_BUFS = 16
 
 FLOPS = 2 * BATCH * TOKENS * (HEADS * QK * DH + GD * INNER + INNER * D_OUT)
 
@@ -34,12 +34,17 @@ def tile_linearattention_pb_t_kernel(
     nc = tc.nc
     with ExitStack() as ctx:
         const = ctx.enter_context(tc.tile_pool(name="const", bufs=1))
-        q_pool = ctx.enter_context(tc.tile_pool(name="q_pool", bufs=CHUNKS))
-        g_pool = ctx.enter_context(tc.tile_pool(name="g_pool", bufs=BATCH))
+        q_pool = ctx.enter_context(tc.tile_pool(name="q_pool", bufs=TILES))
+        g_pool = ctx.enter_context(tc.tile_pool(name="g_pool", bufs=TILES // GROUP))
         work2 = ctx.enter_context(tc.tile_pool(name="work2", bufs=2))
         work3 = ctx.enter_context(tc.tile_pool(name="work3", bufs=3))
+        out_pool = ctx.enter_context(tc.tile_pool(name="out_pool", bufs=OUT_BUFS))
         psum1 = ctx.enter_context(tc.psum_pool(name="psum1", bufs=1))
         psum3 = ctx.enter_context(tc.psum_pool(name="psum3", bufs=3))
+
+        def place(i):
+            b, n = divmod(i, TILES_PER_BATCH)
+            return b, n * P
 
         q_sb = []
         g_sb = []
@@ -49,44 +54,35 @@ def tile_linearattention_pb_t_kernel(
         w_raw = const.tile([P, PACK, D_OUT], BF16)
         bias_bc = const.tile([P, D_OUT], BF16)
 
-        def load_q(c):
-            b, cb = divmod(c, CHUNKS_PER_BATCH)
-            q_chunk = q_pool.tile([P, HEADS, TILES_PER_CHUNK, QK], BF16, name="q_chunk")
-            nc.sync.dma_start(
-                out=q_chunk[:].rearrange("p h j k -> p h (j k)"),
-                in_=q_rot[b, :, cb * CHUNK : (cb + 1) * CHUNK, :].rearrange(
-                    "h (p j) k -> p h (j k)", j=TILES_PER_CHUNK
-                ),
-            )
-            q_sb.append(q_chunk)
-
-        def load_kv_and_g(b):
-            nc.sync.dma_start(
-                out=kv_sb[:, b].rearrange("w h e d -> w h (e d)"),
-                in_=kv[b].rearrange("h (w e) d -> w h (e d)", e=PAIR),
-            )
-            g_batch = g_pool.tile([P, CHUNKS_PER_BATCH, TILES_PER_CHUNK, GD], BF16, name="g_batch")
-            nc.sync.dma_start(
-                out=g_batch[:].rearrange("p c j k -> p c (j k)"),
-                in_=g_low[b].rearrange("(c p j) k -> p c (j k)", p=P, j=TILES_PER_CHUNK),
-            )
-            g_sb.append(g_batch)
-
         nc.vector.memset(ln_rows[:], 0.0)
-
-        load_q(0)
-        load_kv_and_g(0)
-        nc.sync.dma_start(out=w_g2_sb[:], in_=w_g2)
         nc.sync.dma_start(out=ln_rows[0:HEADS, :], in_=ln_gamma.rearrange("(t p) -> t p", p=P))
         nc.sync.dma_start(
             out=ln_rows[HEADS : 2 * HEADS, :], in_=ln_beta.rearrange("(t p) -> t p", p=P)
         )
-        nc.sync.dma_start(out=w_raw[:], in_=w_out.rearrange("(t p) n -> p t n", p=P))
-        nc.sync.dma_start(out=bias_bc[:], in_=b_out.partition_broadcast(P))
-        for c in range(1, CHUNKS):
-            if c % CHUNKS_PER_BATCH == 0:
-                load_kv_and_g(c // CHUNKS_PER_BATCH)
-            load_q(c)
+        for i in range(TILES):
+            b, r = place(i)
+            q_tile = q_pool.tile([P, HEADS, QK], BF16, name="q_tile")
+            nc.sync.dma_start(
+                out=q_tile[:], in_=q_rot[b, :, r : r + P, :].rearrange("h p k -> p h k")
+            )
+            q_sb.append(q_tile)
+            if i % TILES_PER_BATCH == 0:
+                nc.sync.dma_start(
+                    out=kv_sb[:, b].rearrange("w h e d -> w h (e d)"),
+                    in_=kv[b].rearrange("h (w e) d -> w h (e d)", e=PAIR),
+                )
+            if i % GROUP == 0:
+                g_group = g_pool.tile([P, GROUP, GD], BF16, name="g_group")
+                nc.sync.dma_start(
+                    out=g_group[:],
+                    in_=g_low[b, r : r + GROUP * P, :].rearrange("(j p) k -> p j k", p=P),
+                )
+                g_sb.append(g_group)
+            if i == 0:
+                nc.sync.dma_start(out=w_g2_sb[:], in_=w_g2)
+            if i == 1:
+                nc.sync.dma_start(out=w_raw[:], in_=w_out.rearrange("(t p) n -> p t n", p=P))
+                nc.sync.dma_start(out=bias_bc[:], in_=b_out.partition_broadcast(P))
 
         ident_f32 = const.tile([P, P], F32)
         make_identity(nc, ident_f32[:])
@@ -94,52 +90,47 @@ def tile_linearattention_pb_t_kernel(
         make_identity(nc, ident_bf16[:])
         neg_half = const.tile([P, 1], F32)
         nc.vector.memset(neg_half[:], -0.5)
-
-        ln_cols_ps = psum1.tile([P, P], BF16, name="gT_ps")
-        nc.tensor.transpose(ln_cols_ps[:], ln_rows[:], ident_bf16[:])
         ln_cols = const.tile([P, 2 * HEADS], F32)
-        nc.vector.tensor_copy(out=ln_cols[:], in_=ln_cols_ps[:, 0 : 2 * HEADS])
-
         w_grouped = const.tile([P, D_OUT, PACK], BF16, align_bytes=64)
-        nc.vector.tensor_copy(out=w_grouped[:], in_=w_raw[:].rearrange("p t n -> p n t"))
         w_codes = const.tile([P, D_OUT], U32, align_bytes=64)
         w_scales = const.tile([P, D_OUT], U8, align_bytes=64)
-        nc.vector.quantize_mx(
-            out=w_codes[:].bitcast(FP8X4),
-            scales=w_scales[:],
-            in_=w_grouped[:].rearrange("p n t -> p (n t)"),
-        )
+
+        def spread_gamma_beta():
+            ln_cols_ps = psum1.tile([P, P], BF16, name="gT_ps")
+            nc.tensor.transpose(ln_cols_ps[:], ln_rows[:], ident_bf16[:])
+            nc.vector.tensor_copy(out=ln_cols[:], in_=ln_cols_ps[:, 0 : 2 * HEADS])
+
+        def quantise_w_out():
+            nc.vector.tensor_copy(out=w_grouped[:], in_=w_raw[:].rearrange("p t n -> p n t"))
+            nc.vector.quantize_mx(
+                out=w_codes[:].bitcast(FP8X4),
+                scales=w_scales[:],
+                in_=w_grouped[:].rearrange("p n t -> p (n t)"),
+            )
 
         gT_sb, qT_sb, o_ps, stats, mean_var, rstd, shift = {}, {}, {}, {}, {}, {}, {}
-        z_sb, y_sb, gate_sb, h_sb, h_codes, h_scales, out_ps, out_sb = {}, {}, {}, {}, {}, {}, {}, {}
+        z_sb, y_sb, gate_sb, h_sb, h_codes, h_scales, out_ps = {}, {}, {}, {}, {}, {}, {}
 
         def on_scalar(i):
             return i % 2 == 1
 
-        def place(i):
-            c, j = divmod(i, TILES_PER_CHUNK)
-            b, cb = divmod(c, CHUNKS_PER_BATCH)
-            return b, cb, c, j
-
-        def transpose_g(c):
-            b, cb = divmod(c, CHUNKS_PER_BATCH)
-            gT_ps = psum1.tile([P, CHUNK], BF16, name="gT_ps")
-            for j in range(TILES_PER_CHUNK):
-                nc.tensor.transpose(gT_ps[:, j * P : (j + 1) * P], g_sb[b][:, cb, j, :], ident_bf16[:])
-            gT_sb[c] = work2.tile([P, CHUNK], BF16, name="gT")
-            nc.scalar.copy(out=gT_sb[c][:], in_=gT_ps[:])
+        def transpose_g(group):
+            gT_ps = psum1.tile([P, GROUP * P], BF16, name="gT_ps")
+            for j in range(GROUP):
+                nc.tensor.transpose(gT_ps[:, j * P : (j + 1) * P], g_sb[group][:, j, :], ident_bf16[:])
+            gT_sb[group] = work2.tile([P, GROUP * P], BF16, name="gT")
+            nc.scalar.copy(out=gT_sb[group][:], in_=gT_ps[:])
 
         def transpose_q(i):
-            b, cb, c, j = place(i)
-            q_words = q_sb[c][:].bitcast(F32)
+            q_words = q_sb[i][:].bitcast(F32)
             qT_ps = psum1.tile([P, HEADS * P], F32, name="qT_ps")
             for h in range(HEADS):
-                nc.tensor.transpose(qT_ps[:, h * P : (h + 1) * P], q_words[:, h, j, :], ident_f32[:])
+                nc.tensor.transpose(qT_ps[:, h * P : (h + 1) * P], q_words[:, h, :], ident_f32[:])
             qT_sb[i] = work2.tile([P, HEADS * P * PAIR], BF16, name="qT")
             nc.scalar.copy(out=qT_sb[i][:], in_=qT_ps[:].bitcast(BF16))
 
         def attend(i):
-            b, cb, c, j = place(i)
+            b, r = place(i)
             o_ps[i] = psum3.tile([P, INNER], F32, name="o_ps")
             for h in range(HEADS):
                 q_head = qT_sb[i][:, h * P * PAIR : (h + 1) * P * PAIR].rearrange(
@@ -202,13 +193,13 @@ def tile_linearattention_pb_t_kernel(
                 )
 
         def gate(i):
-            b, cb, c, j = place(i)
+            group, j = divmod(i, GROUP)
             gate_ps = psum1.tile([P, HEADS, P], F32, name="gate_ps")
             for t in range(HEADS):
                 nc.tensor.matmul(
                     gate_ps[:, t, :],
                     lhsT=w_g2_sb[:, t * DH : (t + 1) * DH],
-                    rhs=gT_sb[c][:, j * P : (j + 1) * P],
+                    rhs=gT_sb[group][:, j * P : (j + 1) * P],
                     start=True,
                     stop=True,
                 )
@@ -218,9 +209,9 @@ def tile_linearattention_pb_t_kernel(
         def apply_gate(i):
             h_sb[i] = work2.tile([P, P, PACK], BF16, name="h", align_bytes=64)
             nc.vector.tensor_tensor(
-                out=h_sb[i][:].rearrange("p (c r) t -> p c t r", r=4),
-                in0=y_sb[i][:].rearrange("p t (c r) -> p c t r", r=4),
-                in1=gate_sb[i][:].rearrange("p t (c r) -> p c t r", r=4),
+                out=h_sb[i][:].rearrange("p (c r) t -> p c t r", r=RUN),
+                in0=y_sb[i][:].rearrange("p t (c r) -> p c t r", r=RUN),
+                in1=gate_sb[i][:].rearrange("p t (c r) -> p c t r", r=RUN),
                 op=ALU.mult,
             )
 
@@ -245,18 +236,11 @@ def tile_linearattention_pb_t_kernel(
                 stop=True,
             )
 
-        def add_bias(i):
-            b, cb, c, j = place(i)
-            if j == 0:
-                out_sb[c] = work3.tile([P, TILES_PER_CHUNK, D_OUT], F32, name="out_sb")
-            nc.vector.tensor_tensor(out=out_sb[c][:, j, :], in0=out_ps[i][:], in1=bias_bc[:], op=ALU.add)
-            if j == TILES_PER_CHUNK - 1:
-                nc.sync.dma_start(
-                    out=out[b, cb * CHUNK : (cb + 1) * CHUNK, :].rearrange(
-                        "(p j) n -> p (j n)", j=TILES_PER_CHUNK
-                    ),
-                    in_=out_sb[c][:].rearrange("p j n -> p (j n)"),
-                )
+        def add_bias_and_store(i):
+            b, r = place(i)
+            out_sb = out_pool.tile([P, D_OUT], F32, name="out_sb")
+            nc.vector.tensor_tensor(out=out_sb[:], in0=out_ps[i][:], in1=bias_bc[:], op=ALU.add)
+            nc.sync.dma_start(out=out[b, r : r + P, :], in_=out_sb[:])
 
         def run(stage, i):
             if 0 <= i < TILES:
@@ -264,8 +248,12 @@ def tile_linearattention_pb_t_kernel(
 
         with tc.manual_schedule():
             for s in range(TILES + 5):
-                if s < TILES and s % TILES_PER_CHUNK == 0:
-                    transpose_g(s // TILES_PER_CHUNK)
+                if s == 2:
+                    spread_gamma_beta()
+                if s == 3:
+                    quantise_w_out()
+                if s < TILES and s % GROUP == 0:
+                    transpose_g(s // GROUP)
                 run(transpose_q, s)
                 run(attend, s - 1)
                 run(partial_statistics, s - 1)
@@ -277,4 +265,4 @@ def tile_linearattention_pb_t_kernel(
                 run(gate, s - 2)
                 run(project, s - 5)
                 run(quantise, s - 4)
-                run(add_bias, s - 5)
+                run(add_bias_and_store, s - 5)

@@ -112,6 +112,9 @@ def tile_linearattention_pb_t_kernel(
         z_sb, y_sb, gate_sb, h_sb, h_codes, h_scales, out_ps = {}, {}, {}, {}, {}, {}, {}
 
         def on_scalar(i):
+            return i % 4 == 0
+
+        def on_gpsimd(i):
             return i % 2 == 1
 
         def transpose_g(group):
@@ -208,7 +211,8 @@ def tile_linearattention_pb_t_kernel(
 
         def apply_gate(i):
             h_sb[i] = work2.tile([P, P, PACK], BF16, name="h", align_bytes=64)
-            nc.vector.tensor_tensor(
+            engine = nc.gpsimd if on_gpsimd(i) else nc.vector
+            engine.tensor_tensor(
                 out=h_sb[i][:].rearrange("p (c r) t -> p c t r", r=RUN),
                 in0=y_sb[i][:].rearrange("p t (c r) -> p c t r", r=RUN),
                 in1=gate_sb[i][:].rearrange("p t (c r) -> p c t r", r=RUN),
@@ -254,15 +258,15 @@ def tile_linearattention_pb_t_kernel(
                     quantise_w_out()
                 if s < TILES and s % GROUP == 0:
                     transpose_g(s // GROUP)
+                run(quantise, s - 5)
                 run(transpose_q, s)
                 run(attend, s - 1)
                 run(partial_statistics, s - 1)
-                run(apply_gate, s - 4)
                 run(scale_and_shift, s - 3)
                 run(inverse_std, s - 2)
-                run(statistics, s - 1)
                 run(normalise, s - 2)
                 run(gate, s - 2)
+                run(statistics, s - 1)
                 run(project, s - 5)
-                run(quantise, s - 4)
+                run(apply_gate, s - 4)
                 run(add_bias_and_store, s - 5)

from contextlib import ExitStack

import concourse.mybir as mybir
from concourse.masks import make_identity

F32 = mybir.dt.float32
BF16 = mybir.dt.bfloat16
U32 = mybir.dt.uint32
U8 = mybir.dt.uint8
FP8X4 = mybir.dt.float8_e4m3fn_x4
ACT = mybir.ActivationFunctionType
ALU = mybir.AluOpType

P = 128
BATCH, TOKENS, HEADS, QK, DH, GD = 3, 2048, 4, 256, 128, 128
INNER = HEADS * DH
D_OUT = 512
LN_EPS = 1e-5
PACK = 4
PAIR = 2
RUN = 4

TILES_PER_BATCH = TOKENS // P
TILES = BATCH * TILES_PER_BATCH
GROUP = 4
OUT_BUFS = 16

FLOPS = 2 * BATCH * TOKENS * (HEADS * QK * DH + GD * INNER + INNER * D_OUT)


def tile_linearattention_pb_t_kernel(
    tc, q_rot, kv, g_low, w_g2, ln_gamma, ln_beta, w_out, b_out, out
):
    nc = tc.nc
    with ExitStack() as ctx:
        const = ctx.enter_context(tc.tile_pool(name="const", bufs=1))
        q_pool = ctx.enter_context(tc.tile_pool(name="q_pool", bufs=TILES))
        g_pool = ctx.enter_context(tc.tile_pool(name="g_pool", bufs=TILES // GROUP))
        work2 = ctx.enter_context(tc.tile_pool(name="work2", bufs=2))
        work3 = ctx.enter_context(tc.tile_pool(name="work3", bufs=3))
        out_pool = ctx.enter_context(tc.tile_pool(name="out_pool", bufs=OUT_BUFS))
        psum1 = ctx.enter_context(tc.psum_pool(name="psum1", bufs=1))
        psum3 = ctx.enter_context(tc.psum_pool(name="psum3", bufs=3))

        def place(i):
            b, n = divmod(i, TILES_PER_BATCH)
            return b, n * P

        q_sb = []
        g_sb = []
        kv_sb = const.tile([P, BATCH, HEADS, PAIR, DH], BF16)
        w_g2_sb = const.tile([P, INNER], BF16)
        ln_rows = const.tile([P, P], BF16)
        w_raw = const.tile([P, PACK, D_OUT], BF16)
        bias_bc = const.tile([P, D_OUT], BF16)

        nc.vector.memset(ln_rows[:], 0.0)
        nc.sync.dma_start(out=ln_rows[0:HEADS, :], in_=ln_gamma.rearrange("(t p) -> t p", p=P))
        nc.sync.dma_start(
            out=ln_rows[HEADS : 2 * HEADS, :], in_=ln_beta.rearrange("(t p) -> t p", p=P)
        )
        for i in range(TILES):
            b, r = place(i)
            q_tile = q_pool.tile([P, HEADS, QK], BF16, name="q_tile")
            nc.sync.dma_start(
                out=q_tile[:], in_=q_rot[b, :, r : r + P, :].rearrange("h p k -> p h k")
            )
            q_sb.append(q_tile)
            if i % TILES_PER_BATCH == 0:
                nc.sync.dma_start(
                    out=kv_sb[:, b].rearrange("w h e d -> w h (e d)"),
                    in_=kv[b].rearrange("h (w e) d -> w h (e d)", e=PAIR),
                )
            if i % GROUP == 0:
                g_group = g_pool.tile([P, GROUP, GD], BF16, name="g_group")
                nc.sync.dma_start(
                    out=g_group[:],
                    in_=g_low[b, r : r + GROUP * P, :].rearrange("(j p) k -> p j k", p=P),
                )
                g_sb.append(g_group)
            if i == 0:
                nc.sync.dma_start(out=w_g2_sb[:], in_=w_g2)
            if i == 1:
                nc.sync.dma_start(out=w_raw[:], in_=w_out.rearrange("(t p) n -> p t n", p=P))
                nc.sync.dma_start(out=bias_bc[:], in_=b_out.partition_broadcast(P))

        ident_f32 = const.tile([P, P], F32)
        make_identity(nc, ident_f32[:])
        ident_bf16 = const.tile([P, P], BF16)
        make_identity(nc, ident_bf16[:])
        neg_half = const.tile([P, 1], F32)
        nc.vector.memset(neg_half[:], -0.5)
        ln_cols = const.tile([P, 2 * HEADS], F32)
        w_grouped = const.tile([P, D_OUT, PACK], BF16, align_bytes=64)
        w_codes = const.tile([P, D_OUT], U32, align_bytes=64)
        w_scales = const.tile([P, D_OUT], U8, align_bytes=64)

        def spread_gamma_beta():
            ln_cols_ps = psum1.tile([P, P], BF16, name="gT_ps")
            nc.tensor.transpose(ln_cols_ps[:], ln_rows[:], ident_bf16[:])
            nc.vector.tensor_copy(out=ln_cols[:], in_=ln_cols_ps[:, 0 : 2 * HEADS])

        def quantise_w_out():
            nc.vector.tensor_copy(out=w_grouped[:], in_=w_raw[:].rearrange("p t n -> p n t"))
            nc.vector.quantize_mx(
                out=w_codes[:].bitcast(FP8X4),
                scales=w_scales[:],
                in_=w_grouped[:].rearrange("p n t -> p (n t)"),
            )

        gT_sb, qT_sb, o_ps, stats, mean_var, rstd, shift = {}, {}, {}, {}, {}, {}, {}
        z_sb, y_sb, gate_sb, h_sb, h_codes, h_scales, out_ps = {}, {}, {}, {}, {}, {}, {}

        def on_scalar(i):
            return i % 4 == 0

        def on_gpsimd(i):
            return i % 2 == 1

        def transpose_g(group):
            gT_ps = psum1.tile([P, GROUP * P], BF16, name="gT_ps")
            for j in range(GROUP):
                nc.tensor.transpose(gT_ps[:, j * P : (j + 1) * P], g_sb[group][:, j, :], ident_bf16[:])
            gT_sb[group] = work2.tile([P, GROUP * P], BF16, name="gT")
            nc.scalar.copy(out=gT_sb[group][:], in_=gT_ps[:])

        def transpose_q(i):
            q_words = q_sb[i][:].bitcast(F32)
            qT_ps = psum1.tile([P, HEADS * P], F32, name="qT_ps")
            for h in range(HEADS):
                nc.tensor.transpose(qT_ps[:, h * P : (h + 1) * P], q_words[:, h, :], ident_f32[:])
            qT_sb[i] = work2.tile([P, HEADS * P * PAIR], BF16, name="qT")
            nc.scalar.copy(out=qT_sb[i][:], in_=qT_ps[:].bitcast(BF16))

        def attend(i):
            b, r = place(i)
            o_ps[i] = psum3.tile([P, INNER], F32, name="o_ps")
            for h in range(HEADS):
                q_head = qT_sb[i][:, h * P * PAIR : (h + 1) * P * PAIR].rearrange(
                    "w (n e) -> w n e", e=PAIR
                )
                for e in range(PAIR):
                    nc.tensor.matmul(
                        o_ps[i][:, h * DH : (h + 1) * DH],
                        lhsT=q_head[:, :, e],
                        rhs=kv_sb[:, b, h, e, :],
                        start=(e == 0),
                        stop=(e == PAIR - 1),
                    )

        def partial_statistics(i):
            stats[i] = work3.tile([P, 6], F32, name="stats")
            nc.vector.bn_stats(out=stats[i][:], in_=o_ps[i][:])

        def statistics(i):
            mean_var[i] = work3.tile([P, 2], F32, name="mean_var")
            nc.vector.bn_aggr(out=mean_var[i][:], in_=stats[i][:])

        def inverse_std(i):
            var_eps = work3.tile([P, 1], F32, name="var_eps")
            nc.gpsimd.tensor_scalar(
                out=var_eps[:], in0=mean_var[i][:, 1:2], scalar1=LN_EPS, scalar2=1.0,
                op0=ALU.add, op1=ALU.mult,
            )
            rstd[i] = work3.tile([P, 1], F32, name="rstd")
            nc.gpsimd.tensor_tensor(out=rstd[i][:], in0=var_eps[:], in1=neg_half[:], op=ALU.pow)
            if on_scalar(i):
                shift[i] = work3.tile([P, 1], F32, name="shift")
                nc.gpsimd.tensor_scalar(
                    out=shift[i][:], in0=mean_var[i][:, 0:1], scalar1=rstd[i][:], scalar2=-1.0,
                    op0=ALU.mult, op1=ALU.mult,
                )

        def normalise(i):
            z_sb[i] = work2.tile([P, INNER], F32, name="z")
            if on_scalar(i):
                nc.scalar.activation(
                    out=z_sb[i][:], in_=o_ps[i][:], func=ACT.Identity,
                    scale=rstd[i][:], bias=shift[i][:],
                )
            else:
                nc.vector.tensor_scalar(
                    out=z_sb[i][:], in0=o_ps[i][:], scalar1=mean_var[i][:, 0:1], scalar2=rstd[i][:],
                    op0=ALU.subtract, op1=ALU.mult,
                )

        def scale_and_shift(i):
            zT_ps = psum1.tile([P, HEADS, P], F32, name="zT_ps")
            for t in range(HEADS):
                nc.tensor.transpose(zT_ps[:, t, :], z_sb[i][:, t * DH : (t + 1) * DH], ident_f32[:])
            y_sb[i] = work2.tile([P, HEADS, P], F32, name="y")
            for t in range(HEADS):
                nc.scalar.activation(
                    out=y_sb[i][:, t, :], in_=zT_ps[:, t, :], func=ACT.Identity,
                    scale=ln_cols[:, t : t + 1], bias=ln_cols[:, HEADS + t : HEADS + t + 1],
                )

        def gate(i):
            group, j = divmod(i, GROUP)
            gate_ps = psum1.tile([P, HEADS, P], F32, name="gate_ps")
            for t in range(HEADS):
                nc.tensor.matmul(
                    gate_ps[:, t, :],
                    lhsT=w_g2_sb[:, t * DH : (t + 1) * DH],
                    rhs=gT_sb[group][:, j * P : (j + 1) * P],
                    start=True,
                    stop=True,
                )
            gate_sb[i] = work3.tile([P, HEADS, P], F32, name="gate_sb")
            nc.scalar.activation(out=gate_sb[i][:], in_=gate_ps[:], func=ACT.Sigmoid)

        def apply_gate(i):
            h_sb[i] = work2.tile([P, P, PACK], BF16, name="h", align_bytes=64)
            engine = nc.gpsimd if on_gpsimd(i) else nc.vector
            engine.tensor_tensor(
                out=h_sb[i][:].rearrange("p (c r) t -> p c t r", r=RUN),
                in0=y_sb[i][:].rearrange("p t (c r) -> p c t r", r=RUN),
                in1=gate_sb[i][:].rearrange("p t (c r) -> p c t r", r=RUN),
                op=ALU.mult,
            )

        def quantise(i):
            h_codes[i] = work2.tile([P, P], U32, name="h_codes", align_bytes=64)
            h_scales[i] = work2.tile([P, P], U8, name="h_scales", align_bytes=64)
            nc.vector.quantize_mx(
                out=h_codes[i][:].bitcast(FP8X4),
                scales=h_scales[i][:],
                in_=h_sb[i][:].rearrange("p n t -> p (n t)"),
            )

        def project(i):
            out_ps[i] = psum1.tile([P, D_OUT], F32, name="out_ps")
            nc.tensor.matmul_mx(
                out=out_ps[i][:],
                lhsT=h_codes[i][:].bitcast(FP8X4),
                lhsT_scale=h_scales[i][:],
                rhs=w_codes[:].bitcast(FP8X4),
                rhs_scale=w_scales[:],
                start=True,
                stop=True,
            )

        def add_bias_and_store(i):
            b, r = place(i)
            out_sb = out_pool.tile([P, D_OUT], F32, name="out_sb")
            nc.vector.tensor_tensor(out=out_sb[:], in0=out_ps[i][:], in1=bias_bc[:], op=ALU.add)
            nc.sync.dma_start(out=out[b, r : r + P, :], in_=out_sb[:])

        def run(stage, i):
            if 0 <= i < TILES:
                stage(i)

        with tc.manual_schedule():
            for s in range(TILES + 5):
                if s == 2:
                    spread_gamma_beta()
                if s == 3:
                    quantise_w_out()
                if s < TILES and s % GROUP == 0:
                    transpose_g(s // GROUP)
                run(quantise, s - 5)
                run(transpose_q, s)
                run(attend, s - 1)
                run(partial_statistics, s - 1)
                run(scale_and_shift, s - 3)
                run(inverse_std, s - 2)
                run(normalise, s - 2)
                run(gate, s - 2)
                run(statistics, s - 1)
                run(project, s - 5)
                run(apply_gate, s - 4)
                run(add_bias_and_store, s - 5)
